import numpy as np
import ml_dtypes


def mxq(x, axis, fmt="e4m3"):
    dtype, down = {"e4m3": (ml_dtypes.float8_e4m3fn, 7), "e5m2": (ml_dtypes.float8_e5m2, 14)}[fmt]
    v = np.moveaxis(np.asarray(x, np.float32).astype(ml_dtypes.bfloat16).astype(np.float64), axis, -1)
    blocks = v.reshape(v.shape[:-1] + (-1, 32))
    amax = np.abs(blocks).max(-1, keepdims=True)
    byte = np.maximum(np.where(amax > 0, np.frexp(amax)[1] - 1 + 127, 0) - down, 1)
    scale = np.exp2(byte - 127.0)
    codes = (blocks / scale).astype(np.float32).astype(dtype).astype(np.float64)
    return np.moveaxis((codes * scale).reshape(v.shape), -1, axis)


WIDE = False


def mx_kscale(k):
    if not WIDE:
        return np.ones(k)
    levels = np.array([10, -10, 5, -5, 0])
    a = np.random.permutation(np.resize(levels, k // 512 * 4)).reshape(k // 512, 4)
    idx = np.arange(k)
    return np.exp2(a[idx // 512, idx % 128 // 32])


BF16 = ml_dtypes.bfloat16


def bf(x):
    return np.asarray(x, np.float32).astype(BF16)


def f64(x):
    return np.asarray(x).astype(np.float64)


B, S, HID, H, G, D, QB = 4, 2048, 1024, 2, 1, 128, 512
ROPE_THETA = 1.0e6


def rotate_half(t):
    t1 = t[..., t.shape[-1] // 2:]
    t2 = t[..., : t.shape[-1] // 2]
    return np.concatenate((-t1, t2), axis=-1)


def rope_tables():
    inv_freq = 1.0 / (ROPE_THETA ** (np.arange(0, D, 2) / D))
    freqs = np.arange(S)[:, None] * inv_freq[None, :]
    emb = np.concatenate((freqs, freqs), axis=-1)
    return np.cos(emb), np.sin(emb)


def setup_inputs():
    s = mx_kscale(HID)
    cos, sin = rope_tables()
    return {"x": bf(np.random.standard_normal((B, S, HID)) * s),
            "cos": bf(cos),
            "sin": bf(sin),
            "Wq": bf(np.random.standard_normal((HID, H * D)) * 1.5 / np.sqrt(HID) / s[:, None]),
            "Wk": bf(np.random.standard_normal((HID, G * D)) * 1.5 / np.sqrt(HID) / s[:, None]),
            "Wv": bf(np.random.standard_normal((HID, G * D)) * 1.0 / np.sqrt(HID) / s[:, None])}


def reference(x, cos, sin, Wq, Wk, Wv):
    xq = mxq(f64(x), 2, "e4m3")
    q = (xq @ mxq(f64(Wq), 0, "e4m3")).reshape(B, S, H, D)
    k = (xq @ mxq(f64(Wk), 0, "e4m3")).reshape(B, S, G, D)
    v = (xq @ mxq(f64(Wv), 0, "e4m3")).reshape(B, S, G, D)
    c = f64(cos)[None, :, None, :]
    sn = f64(sin)[None, :, None, :]
    q = q * c + rotate_half(q) * sn
    k = k * c + rotate_half(k) * sn
    return q, k, v

@@ -1,0 +1,229 @@
+from contextlib import ExitStack
+
+import concourse.mybir as mybir
+from concourse.masks import make_identity
+
+F32 = mybir.dt.float32
+BF16 = mybir.dt.bfloat16
+U32 = mybir.dt.uint32
+U8 = mybir.dt.uint8
+FP8X4 = mybir.dt.float8_e4m3fn_x4
+ALU = mybir.AluOpType
+
+P = 128
+BATCH, SEQ, HID = 4, 2048, 1024
+HEAD = 128
+HALF = HEAD // 2
+Q_HEADS = 2
+Q_COLS, K_COLS, V_COLS = Q_HEADS * HEAD, HEAD, HEAD
+OUT_COLS = Q_COLS + K_COLS + V_COLS
+K_FIRST, V_FIRST = Q_COLS, Q_COLS + K_COLS
+
+PACK = 4
+PASSES = HID // (P * PACK)
+PAIR = 2
+
+TILES = 4
+CHUNKS = BATCH * SEQ // (TILES * P)
+SEQ_CHUNKS = SEQ // (TILES * P)
+Q_TILES = 2
+
+LOAD_AHEAD = 4
+X_BUFS = LOAD_AHEAD + 2
+
+FLOPS = 2 * BATCH * SEQ * HID * OUT_COLS
+
+
+def tile_attention_pa_t_kernel(tc, x, cos, sin, Wq, Wk, Wv, out_0, out_1, out_2):
+    nc = tc.nc
+
+    by_chunk = "(c p j) n -> c p (j n)"
+    x_chunks = x.flatten_outer_dims().rearrange(by_chunk, p=P, j=TILES)
+    q_chunks = out_0.rearrange("b s h d -> (b s) (h d)").rearrange(by_chunk, p=P, j=TILES)
+    k_chunks = out_1.rearrange("b s h d -> (b s) (h d)").rearrange(by_chunk, p=P, j=TILES)
+    v_chunks = out_2.rearrange("b s h d -> (b s) (h d)").rearrange(by_chunk, p=P, j=TILES)
+
+    with ExitStack() as stack:
+        stack.enter_context(tc.manual_schedule())
+        const = stack.enter_context(tc.tile_pool(name="const", bufs=1))
+        x_pool = stack.enter_context(tc.tile_pool(name="x", bufs=X_BUFS))
+        mx_pool = stack.enter_context(tc.tile_pool(name="mx", bufs=2))
+        cross_pool = stack.enter_context(tc.tile_pool(name="cross", bufs=2))
+        out_pool = stack.enter_context(tc.tile_pool(name="out", bufs=3))
+        xt_psum = stack.enter_context(tc.psum_pool(name="xt_psum", bufs=TILES))
+        q_psum = stack.enter_context(tc.psum_pool(name="q_psum", bufs=2))
+        kv_psum = stack.enter_context(tc.psum_pool(name="kv_psum", bufs=1))
+
+        x_tiles, grouped_tiles, code_tiles, scale_tiles, product_tiles = {}, {}, {}, {}, {}
+
+        def load(c):
+            x_sb = x_pool.tile([P, TILES * HID], BF16, name="x_sb")
+            nc.sync.dma_start(out=x_sb[:], in_=x_chunks[c])
+            x_tiles[c] = x_sb
+
+        def transpose(c):
+            x_words = x_tiles[c][:].bitcast(F32)
+            grouped = mx_pool.tile([P, TILES * HID], BF16, name="grouped", align_bytes=64)
+            grouped_words = grouped[:].bitcast(F32).rearrange(
+                "p (j g r u) -> p j g r u", j=TILES, g=PASSES, u=PAIR
+            )
+            for j in range(TILES):
+                xt = xt_psum.tile([P, PASSES, PAIR, P], F32, name="xt")
+                for g in range(PASSES):
+                    for u in range(PAIR):
+                        first = ((j * PASSES + g) * PAIR + u) * P
+                        nc.tensor.transpose(
+                            out=xt[:, g, u, :], in_=x_words[:, first : first + P], identity=ident[:]
+                        )
+                nc.scalar.copy(out=grouped_words[:, j], in_=xt[:].rearrange("p g u r -> p g r u"))
+            grouped_tiles[c] = grouped
+
+        def quantise(c):
+            x_codes = mx_pool.tile([P, TILES * PASSES * P], U32, name="x_codes", align_bytes=64)
+            x_scales = mx_pool.tile([P, TILES * PASSES * P], U8, name="x_scales", align_bytes=64)
+            nc.vector.quantize_mx(
+                out=x_codes[:].bitcast(FP8X4), scales=x_scales[:], in_=grouped_tiles[c][:]
+            )
+            code_tiles[c], scale_tiles[c] = x_codes, x_scales
+
+        def multiply(c, j, w_first, w_cols, acc):
+            for g in range(PASSES):
+                tokens = slice((j * PASSES + g) * P, (j * PASSES + g + 1) * P)
+                columns = slice(g * OUT_COLS + w_first, g * OUT_COLS + w_first + w_cols)
+                nc.tensor.matmul_mx(
+                    out=acc,
+                    lhsT=code_tiles[c][:, tokens].bitcast(FP8X4),
+                    lhsT_scale=scale_tiles[c][:, tokens],
+                    rhs=w_codes[:, columns].bitcast(FP8X4),
+                    rhs_scale=w_scales[:, columns],
+                    start=(g == 0),
+                    stop=(g == PASSES - 1),
+                )
+
+        def project(c):
+            q_accs = []
+            for b in range(TILES // Q_TILES):
+                q_acc = q_psum.tile([P, Q_TILES, Q_HEADS, HEAD], F32, name="q_acc")
+                for i in range(Q_TILES):
+                    multiply(c, b * Q_TILES + i, 0, Q_COLS, q_acc[:, i].rearrange("p h d -> p (h d)"))
+                q_accs.append(q_acc)
+            k_acc = kv_psum.tile([P, TILES, HEAD], F32, name="k_acc")
+            for j in range(TILES):
+                multiply(c, j, K_FIRST, K_COLS, k_acc[:, j, :])
+            v_acc = kv_psum.tile([P, TILES, HEAD], F32, name="v_acc")
+            for j in range(TILES):
+                multiply(c, j, V_FIRST, V_COLS, v_acc[:, j, :])
+            v_out = out_pool.tile([P, TILES, HEAD], F32, name="v_out")
+            nc.scalar.copy(out=v_out[:], in_=v_acc[:])
+            product_tiles[c] = (q_accs, k_acc, v_out)
+
+        def add_exchanged(rot, cross):
+            nc.gpsimd.tensor_tensor(
+                out=rot[:, :, 0, :], in0=rot[:, :, 0, :], in1=cross[:, :, 1, :], op=ALU.subtract
+            )
+            nc.gpsimd.tensor_tensor(
+                out=rot[:, :, 1, :], in0=rot[:, :, 1, :], in1=cross[:, :, 0, :], op=ALU.add
+            )
+
+        def rotate_and_store(c):
+            q_accs, k_acc, v_out = product_tiles[c]
+            table_first = (c % SEQ_CHUNKS) * TILES
+
+            q_rot = out_pool.tile([P, TILES, Q_HEADS, HEAD], F32, name="q_rot")
+            q_cross = cross_pool.tile([P, TILES, Q_HEADS, HEAD], F32, name="q_cross")
+            for b in range(TILES // Q_TILES):
+                tiles = slice(b * Q_TILES, (b + 1) * Q_TILES)
+                rows = slice(table_first + b * Q_TILES, table_first + (b + 1) * Q_TILES)
+                both_heads = [P, Q_TILES, Q_HEADS, HEAD]
+                nc.vector.tensor_tensor(
+                    out=q_rot[:, tiles],
+                    in0=q_accs[b][:],
+                    in1=cos_sb[:, rows, :].unsqueeze(2).to_broadcast(both_heads),
+                    op=ALU.mult,
+                )
+                nc.vector.tensor_tensor(
+                    out=q_cross[:, tiles],
+                    in0=q_accs[b][:],
+                    in1=sin_swapped[:, rows, :].unsqueeze(2).to_broadcast(both_heads),
+                    op=ALU.mult,
+                )
+            add_exchanged(
+                q_rot[:].rearrange("p j h (f d) -> p (j h) f d", f=2),
+                q_cross[:].rearrange("p j h (f d) -> p (j h) f d", f=2),
+            )
+            nc.sync.dma_start(out=q_chunks[c], in_=q_rot[:].rearrange("p j h d -> p (j h d)"))
+
+            k_rot = out_pool.tile([P, TILES, HEAD], F32, name="k_rot")
+            k_cross = cross_pool.tile([P, TILES, HEAD], F32, name="k_cross")
+            rows = slice(table_first, table_first + TILES)
+            nc.vector.tensor_tensor(out=k_rot[:], in0=k_acc[:], in1=cos_sb[:, rows, :], op=ALU.mult)
+            nc.vector.tensor_tensor(
+                out=k_cross[:], in0=k_acc[:], in1=sin_swapped[:, rows, :], op=ALU.mult
+            )
+            add_exchanged(
+                k_rot[:].rearrange("p j (f d) -> p j f d", f=2),
+                k_cross[:].rearrange("p j (f d) -> p j f d", f=2),
+            )
+            nc.sync.dma_start(out=k_chunks[c], in_=k_rot[:].rearrange("p j d -> p (j d)"))
+            nc.sync.dma_start(out=v_chunks[c], in_=v_out[:].rearrange("p j d -> p (j d)"))
+
+        ident = const.tile([P, P], F32)
+        make_identity(nc, ident[:])
+
+        w_raws = []
+        for name, w in (("wq_raw", Wq), ("wk_raw", Wk), ("wv_raw", Wv)):
+            w_raw = const.tile([P, PASSES, PACK, w.shape[1]], BF16, name=name)
+            nc.sync.dma_start(
+                out=w_raw[:].rearrange("p g (u e) n -> p (g u) (e n)", e=PAIR),
+                in_=w.rearrange("(s q e) n -> q s (e n)", q=P, e=PAIR),
+            )
+            w_raws.append((w_raw, w.shape[1]))
+
+        load(0)
+
+        by_partition = "(c p j) d -> p c (j d)"
+        cos_sb = const.tile([P, SEQ_CHUNKS * TILES, HEAD], BF16)
+        sin_sb = const.tile([P, SEQ_CHUNKS * TILES, HEAD], BF16)
+        for table_sb, table in ((sin_sb, sin), (cos_sb, cos)):
+            nc.sync.dma_start(
+                out=table_sb[:].rearrange("p (c j) d -> p c (j d)", j=TILES),
+                in_=table.rearrange(by_partition, p=P, j=TILES),
+            )
+
+        for c in range(1, LOAD_AHEAD):
+            load(c)
+
+        w_grouped = const.tile([P, PASSES, OUT_COLS, PACK], BF16, align_bytes=64)
+        w_first = 0
+        for w_raw, w_cols in w_raws:
+            for g in range(PASSES):
+                nc.vector.tensor_copy(
+                    out=w_grouped[:, g, w_first : w_first + w_cols, :],
+                    in_=w_raw[:, g].rearrange("p t n -> p n t"),
+                )
+            w_first += w_cols
+        w_codes = const.tile([P, PASSES * OUT_COLS], U32, align_bytes=64)
+        w_scales = const.tile([P, PASSES * OUT_COLS], U8, align_bytes=64)
+        nc.vector.quantize_mx(
+            out=w_codes[:].bitcast(FP8X4),
+            scales=w_scales[:],
+            in_=w_grouped[:].rearrange("p g n t -> p (g n t)"),
+        )
+
+        transpose(0)
+        transpose(1)
+
+        sin_swapped = const.tile([P, SEQ_CHUNKS * TILES, HEAD], BF16)
+        nc.scalar.copy(out=sin_swapped[:, :, 0:HALF], in_=sin_sb[:, :, HALF:HEAD])
+        nc.scalar.copy(out=sin_swapped[:, :, HALF:HEAD], in_=sin_sb[:, :, 0:HALF])
+
+        quantise(0)
+        for c in range(CHUNKS):
+            if c + LOAD_AHEAD < CHUNKS:
+                load(c + LOAD_AHEAD)
+            if c + 1 < CHUNKS:
+                quantise(c + 1)
+            project(c)
+            if c + 2 < CHUNKS:
+                transpose(c + 2)
+            rotate_and_store(c)

@@ -27,6 +27,8 @@ TILES = 4
 CHUNKS = BATCH * SEQ // (TILES * P)
 SEQ_CHUNKS = SEQ // (TILES * P)
 Q_TILES = 2
+K_HEAD_FIRST = TILES * Q_HEADS
+ROT_HEADS = K_HEAD_FIRST + TILES
 
 LOAD_AHEAD = 4
 X_BUFS = LOAD_AHEAD + 2
@@ -117,54 +119,53 @@ def tile_attention_pa_t_kernel(tc, x, cos, sin, Wq, Wk, Wv, out_0, out_1, out_2)
             nc.scalar.copy(out=v_out[:], in_=v_acc[:])
             product_tiles[c] = (q_accs, k_acc, v_out)
 
-        def add_exchanged(rot, cross):
-            nc.gpsimd.tensor_tensor(
-                out=rot[:, :, 0, :], in0=rot[:, :, 0, :], in1=cross[:, :, 1, :], op=ALU.subtract
-            )
-            nc.gpsimd.tensor_tensor(
-                out=rot[:, :, 1, :], in0=rot[:, :, 1, :], in1=cross[:, :, 0, :], op=ALU.add
-            )
-
         def rotate_and_store(c):
             q_accs, k_acc, v_out = product_tiles[c]
             table_first = (c % SEQ_CHUNKS) * TILES
 
-            q_rot = out_pool.tile([P, TILES, Q_HEADS, HEAD], F32, name="q_rot")
-            q_cross = cross_pool.tile([P, TILES, Q_HEADS, HEAD], F32, name="q_cross")
+            rot = out_pool.tile([P, ROT_HEADS, HEAD], F32, name="rot")
+            cross = cross_pool.tile([P, ROT_HEADS, HEAD], F32, name="cross")
             for b in range(TILES // Q_TILES):
-                tiles = slice(b * Q_TILES, (b + 1) * Q_TILES)
+                heads = slice(b * Q_TILES * Q_HEADS, (b + 1) * Q_TILES * Q_HEADS)
                 rows = slice(table_first + b * Q_TILES, table_first + (b + 1) * Q_TILES)
                 both_heads = [P, Q_TILES, Q_HEADS, HEAD]
-                nc.vector.tensor_tensor(
-                    out=q_rot[:, tiles],
-                    in0=q_accs[b][:],
-                    in1=cos_sb[:, rows, :].unsqueeze(2).to_broadcast(both_heads),
-                    op=ALU.mult,
-                )
-                nc.vector.tensor_tensor(
-                    out=q_cross[:, tiles],
-                    in0=q_accs[b][:],
-                    in1=sin_swapped[:, rows, :].unsqueeze(2).to_broadcast(both_heads),
-                    op=ALU.mult,
-                )
-            add_exchanged(
-                q_rot[:].rearrange("p j h (f d) -> p (j h) f d", f=2),
-                q_cross[:].rearrange("p j h (f d) -> p (j h) f d", f=2),
-            )
-            nc.sync.dma_start(out=q_chunks[c], in_=q_rot[:].rearrange("p j h d -> p (j h d)"))
-
-            k_rot = out_pool.tile([P, TILES, HEAD], F32, name="k_rot")
-            k_cross = cross_pool.tile([P, TILES, HEAD], F32, name="k_cross")
+                for table_sb, product in ((cos_sb, rot), (sin_swapped, cross)):
+                    nc.vector.tensor_tensor(
+                        out=product[:, heads, :].rearrange("p (j h) d -> p j h d", h=Q_HEADS),
+                        in0=q_accs[b][:],
+                        in1=table_sb[:, rows, :].unsqueeze(2).to_broadcast(both_heads),
+                        op=ALU.mult,
+                    )
             rows = slice(table_first, table_first + TILES)
-            nc.vector.tensor_tensor(out=k_rot[:], in0=k_acc[:], in1=cos_sb[:, rows, :], op=ALU.mult)
-            nc.vector.tensor_tensor(
-                out=k_cross[:], in0=k_acc[:], in1=sin_swapped[:, rows, :], op=ALU.mult
+            for table_sb, product in ((cos_sb, rot), (sin_swapped, cross)):
+                nc.vector.tensor_tensor(
+                    out=product[:, K_HEAD_FIRST:ROT_HEADS, :],
+                    in0=k_acc[:],
+                    in1=table_sb[:, rows, :],
+                    op=ALU.mult,
+                )
+
+            rot_halves = rot[:].rearrange("p n (f d) -> p n f d", f=2)
+            cross_halves = cross[:].rearrange("p n (f d) -> p n f d", f=2)
+            nc.gpsimd.tensor_tensor(
+                out=rot_halves[:, :, 0, :],
+                in0=rot_halves[:, :, 0, :],
+                in1=cross_halves[:, :, 1, :],
+                op=ALU.subtract,
             )
-            add_exchanged(
-                k_rot[:].rearrange("p j (f d) -> p j f d", f=2),
-                k_cross[:].rearrange("p j (f d) -> p j f d", f=2),
+            nc.gpsimd.tensor_tensor(
+                out=rot_halves[:, :, 1, :],
+                in0=rot_halves[:, :, 1, :],
+                in1=cross_halves[:, :, 0, :],
+                op=ALU.add,
             )
-            nc.sync.dma_start(out=k_chunks[c], in_=k_rot[:].rearrange("p j d -> p (j d)"))
+
+            nc.sync.dma_start(
+                out=q_chunks[c], in_=rot[:, 0:K_HEAD_FIRST, :].rearrange("p n d -> p (n d)")
+            )
+            nc.sync.dma_start(
+                out=k_chunks[c], in_=rot[:, K_HEAD_FIRST:ROT_HEADS, :].rearrange("p n d -> p (n d)")
+            )
             nc.sync.dma_start(out=v_chunks[c], in_=v_out[:].rearrange("p j d -> p (j d)"))
 
         ident = const.tile([P, P], F32)

@@ -15,9 +15,9 @@ BATCH, SEQ, HID = 4, 2048, 1024
 HEAD = 128
 HALF = HEAD // 2
 Q_HEADS = 2
-Q_COLS, K_COLS, V_COLS = Q_HEADS * HEAD, HEAD, HEAD
-OUT_COLS = Q_COLS + K_COLS + V_COLS
-K_FIRST, V_FIRST = Q_COLS, Q_COLS + K_COLS
+ROT_HEADS = Q_HEADS + 1
+HEADS = ROT_HEADS + 1
+OUT_COLS = HEADS * HEAD
 
 PACK = 4
 PASSES = HID // (P * PACK)
@@ -26,9 +26,8 @@ PAIR = 2
 TILES = 4
 CHUNKS = BATCH * SEQ // (TILES * P)
 SEQ_CHUNKS = SEQ // (TILES * P)
-Q_TILES = 2
-K_HEAD_FIRST = TILES * Q_HEADS
-ROT_HEADS = K_HEAD_FIRST + TILES
+Q_VECTORS = TILES * Q_HEADS
+ROT_VECTORS = TILES * ROT_HEADS
 
 LOAD_AHEAD = 4
 X_BUFS = LOAD_AHEAD + 2
@@ -50,17 +49,18 @@ def tile_attention_pa_t_kernel(tc, x, cos, sin, Wq, Wk, Wv, out_0, out_1, out_2)
         const = stack.enter_context(tc.tile_pool(name="const", bufs=1))
         x_pool = stack.enter_context(tc.tile_pool(name="x", bufs=X_BUFS))
         mx_pool = stack.enter_context(tc.tile_pool(name="mx", bufs=2))
-        cross_pool = stack.enter_context(tc.tile_pool(name="cross", bufs=2))
         out_pool = stack.enter_context(tc.tile_pool(name="out", bufs=3))
         xt_psum = stack.enter_context(tc.psum_pool(name="xt_psum", bufs=TILES))
-        q_psum = stack.enter_context(tc.psum_pool(name="q_psum", bufs=2))
-        kv_psum = stack.enter_context(tc.psum_pool(name="kv_psum", bufs=1))
+        head_psum = stack.enter_context(tc.psum_pool(name="head_psum", bufs=1))
 
-        x_tiles, grouped_tiles, code_tiles, scale_tiles, product_tiles = {}, {}, {}, {}, {}
+        x_tiles, grouped_tiles, code_tiles, scale_tiles, head_tiles = {}, {}, {}, {}, {}
 
-        def load(c):
+        def load(c, pieces=1):
             x_sb = x_pool.tile([P, TILES * HID], BF16, name="x_sb")
-            nc.sync.dma_start(out=x_sb[:], in_=x_chunks[c])
+            width = TILES * HID // pieces
+            for i in range(pieces):
+                columns = slice(i * width, (i + 1) * width)
+                nc.sync.dma_start(out=x_sb[:, columns], in_=x_chunks[c][:, columns])
             x_tiles[c] = x_sb
 
         def transpose(c):
@@ -88,85 +88,55 @@ def tile_attention_pa_t_kernel(tc, x, cos, sin, Wq, Wk, Wv, out_0, out_1, out_2)
             )
             code_tiles[c], scale_tiles[c] = x_codes, x_scales
 
-        def multiply(c, j, w_first, w_cols, acc):
-            for g in range(PASSES):
-                tokens = slice((j * PASSES + g) * P, (j * PASSES + g + 1) * P)
-                columns = slice(g * OUT_COLS + w_first, g * OUT_COLS + w_first + w_cols)
-                nc.tensor.matmul_mx(
-                    out=acc,
-                    lhsT=code_tiles[c][:, tokens].bitcast(FP8X4),
-                    lhsT_scale=scale_tiles[c][:, tokens],
-                    rhs=w_codes[:, columns].bitcast(FP8X4),
-                    rhs_scale=w_scales[:, columns],
-                    start=(g == 0),
-                    stop=(g == PASSES - 1),
-                )
-
-        def project(c):
-            q_accs = []
-            for b in range(TILES // Q_TILES):
-                q_acc = q_psum.tile([P, Q_TILES, Q_HEADS, HEAD], F32, name="q_acc")
-                for i in range(Q_TILES):
-                    multiply(c, b * Q_TILES + i, 0, Q_COLS, q_acc[:, i].rearrange("p h d -> p (h d)"))
-                q_accs.append(q_acc)
-            k_acc = kv_psum.tile([P, TILES, HEAD], F32, name="k_acc")
+        def project(c, h):
+            acc = head_psum.tile([P, TILES, HEAD], F32, name="head%d" % h)
             for j in range(TILES):
-                multiply(c, j, K_FIRST, K_COLS, k_acc[:, j, :])
-            v_acc = kv_psum.tile([P, TILES, HEAD], F32, name="v_acc")
-            for j in range(TILES):
-                multiply(c, j, V_FIRST, V_COLS, v_acc[:, j, :])
-            v_out = out_pool.tile([P, TILES, HEAD], F32, name="v_out")
-            nc.scalar.copy(out=v_out[:], in_=v_acc[:])
-            product_tiles[c] = (q_accs, k_acc, v_out)
+                for g in range(PASSES):
+                    tokens = slice((j * PASSES + g) * P, (j * PASSES + g + 1) * P)
+                    columns = slice(g * OUT_COLS + h * HEAD, g * OUT_COLS + (h + 1) * HEAD)
+                    nc.tensor.matmul_mx(
+                        out=acc[:, j, :],
+                        lhsT=code_tiles[c][:, tokens].bitcast(FP8X4),
+                        lhsT_scale=scale_tiles[c][:, tokens],
+                        rhs=w_codes[:, columns].bitcast(FP8X4),
+                        rhs_scale=w_scales[:, columns],
+                        start=(g == 0),
+                        stop=(g == PASSES - 1),
+                    )
+            head_tiles[c, h] = acc
 
         def rotate_and_store(c):
-            q_accs, k_acc, v_out = product_tiles[c]
-            table_first = (c % SEQ_CHUNKS) * TILES
+            v_out = out_pool.tile([P, TILES, HEAD], F32, name="v_out")
+            nc.scalar.copy(out=v_out[:], in_=head_tiles[c, ROT_HEADS][:])
+            nc.sync.dma_start(out=v_chunks[c], in_=v_out[:].rearrange("p j d -> p (j d)"))
 
-            rot = out_pool.tile([P, ROT_HEADS, HEAD], F32, name="rot")
-            cross = cross_pool.tile([P, ROT_HEADS, HEAD], F32, name="cross")
-            for b in range(TILES // Q_TILES):
-                heads = slice(b * Q_TILES * Q_HEADS, (b + 1) * Q_TILES * Q_HEADS)
-                rows = slice(table_first + b * Q_TILES, table_first + (b + 1) * Q_TILES)
-                both_heads = [P, Q_TILES, Q_HEADS, HEAD]
-                for table_sb, product in ((cos_sb, rot), (sin_swapped, cross)):
-                    nc.vector.tensor_tensor(
-                        out=product[:, heads, :].rearrange("p (j h) d -> p j h d", h=Q_HEADS),
-                        in0=q_accs[b][:],
-                        in1=table_sb[:, rows, :].unsqueeze(2).to_broadcast(both_heads),
-                        op=ALU.mult,
-                    )
-            rows = slice(table_first, table_first + TILES)
-            for table_sb, product in ((cos_sb, rot), (sin_swapped, cross)):
+            products = out_pool.tile([P, 2, ROT_VECTORS, HEAD], F32, name="products")
+            q_products = products[:, :, 0:Q_VECTORS, :].rearrange("p w (j h) d -> p w j h d", h=Q_HEADS)
+            first = (c % SEQ_CHUNKS) * TILES
+            for h in range(ROT_HEADS):
                 nc.vector.tensor_tensor(
-                    out=product[:, K_HEAD_FIRST:ROT_HEADS, :],
-                    in0=k_acc[:],
-                    in1=table_sb[:, rows, :],
+                    out=(
+                        q_products[:, :, :, h, :]
+                        if h < Q_HEADS
+                        else products[:, :, Q_VECTORS:ROT_VECTORS, :]
+                    ),
+                    in0=head_tiles[c, h][:].unsqueeze(1).to_broadcast([P, 2, TILES, HEAD]),
+                    in1=tables[:, :, first : first + TILES, :],
                     op=ALU.mult,
                 )
 
-            rot_halves = rot[:].rearrange("p n (f d) -> p n f d", f=2)
-            cross_halves = cross[:].rearrange("p n (f d) -> p n f d", f=2)
-            nc.gpsimd.tensor_tensor(
-                out=rot_halves[:, :, 0, :],
-                in0=rot_halves[:, :, 0, :],
-                in1=cross_halves[:, :, 1, :],
-                op=ALU.subtract,
+            adder = nc.gpsimd if c < CHUNKS - 1 else nc.vector
+            rot, cross = products[:, 0], products[:, 1]
+            adder.tensor_tensor(
+                out=rot[:, :, 0:HALF], in0=rot[:, :, 0:HALF], in1=cross[:, :, HALF:HEAD], op=ALU.subtract
             )
-            nc.gpsimd.tensor_tensor(
-                out=rot_halves[:, :, 1, :],
-                in0=rot_halves[:, :, 1, :],
-                in1=cross_halves[:, :, 0, :],
-                op=ALU.add,
+            adder.tensor_tensor(
+                out=rot[:, :, HALF:HEAD], in0=rot[:, :, HALF:HEAD], in1=cross[:, :, 0:HALF], op=ALU.add
             )
-
+            nc.sync.dma_start(out=q_chunks[c], in_=rot[:, 0:Q_VECTORS, :].rearrange("p n d -> p (n d)"))
             nc.sync.dma_start(
-                out=q_chunks[c], in_=rot[:, 0:K_HEAD_FIRST, :].rearrange("p n d -> p (n d)")
+                out=k_chunks[c], in_=rot[:, Q_VECTORS:ROT_VECTORS, :].rearrange("p n d -> p (n d)")
             )
-            nc.sync.dma_start(
-                out=k_chunks[c], in_=rot[:, K_HEAD_FIRST:ROT_HEADS, :].rearrange("p n d -> p (n d)")
-            )
-            nc.sync.dma_start(out=v_chunks[c], in_=v_out[:].rearrange("p j d -> p (j d)"))
 
         ident = const.tile([P, P], F32)
         make_identity(nc, ident[:])
@@ -180,15 +150,14 @@ def tile_attention_pa_t_kernel(tc, x, cos, sin, Wq, Wk, Wv, out_0, out_1, out_2)
             )
             w_raws.append((w_raw, w.shape[1]))
 
-        load(0)
+        load(0, pieces=TILES)
 
-        by_partition = "(c p j) d -> p c (j d)"
-        cos_sb = const.tile([P, SEQ_CHUNKS * TILES, HEAD], BF16)
+        tables = const.tile([P, 2, SEQ_CHUNKS * TILES, HEAD], BF16)
         sin_sb = const.tile([P, SEQ_CHUNKS * TILES, HEAD], BF16)
-        for table_sb, table in ((sin_sb, sin), (cos_sb, cos)):
+        for table_sb, table in ((sin_sb[:], sin), (tables[:, 0], cos)):
             nc.sync.dma_start(
-                out=table_sb[:].rearrange("p (c j) d -> p c (j d)", j=TILES),
-                in_=table.rearrange(by_partition, p=P, j=TILES),
+                out=table_sb.rearrange("p (c j) d -> p c (j d)", j=TILES),
+                in_=table.rearrange("(c p j) d -> p c (j d)", p=P, j=TILES),
             )
 
         for c in range(1, LOAD_AHEAD):
@@ -214,9 +183,8 @@ def tile_attention_pa_t_kernel(tc, x, cos, sin, Wq, Wk, Wv, out_0, out_1, out_2)
         transpose(0)
         transpose(1)
 
-        sin_swapped = const.tile([P, SEQ_CHUNKS * TILES, HEAD], BF16)
-        nc.scalar.copy(out=sin_swapped[:, :, 0:HALF], in_=sin_sb[:, :, HALF:HEAD])
-        nc.scalar.copy(out=sin_swapped[:, :, HALF:HEAD], in_=sin_sb[:, :, 0:HALF])
+        nc.scalar.copy(out=tables[:, 1, :, 0:HALF], in_=sin_sb[:, :, HALF:HEAD])
+        nc.scalar.copy(out=tables[:, 1, :, HALF:HEAD], in_=sin_sb[:, :, 0:HALF])
 
         quantise(0)
         for c in range(CHUNKS):
@@ -224,7 +192,10 @@ def tile_attention_pa_t_kernel(tc, x, cos, sin, Wq, Wk, Wv, out_0, out_1, out_2)
                 load(c + LOAD_AHEAD)
             if c + 1 < CHUNKS:
                 quantise(c + 1)
-            project(c)
+            for h in range(Q_HEADS):
+                project(c, h)
             if c + 2 < CHUNKS:
                 transpose(c + 2)
+            for h in range(Q_HEADS, HEADS):
+                project(c, h)
             rotate_and_store(c)

from contextlib import ExitStack

import concourse.mybir as mybir
from concourse.masks import make_identity

F32 = mybir.dt.float32
BF16 = mybir.dt.bfloat16
U32 = mybir.dt.uint32
U8 = mybir.dt.uint8
FP8X4 = mybir.dt.float8_e4m3fn_x4
ALU = mybir.AluOpType

P = 128
BATCH, SEQ, HID = 4, 2048, 1024
HEAD = 128
HALF = HEAD // 2
Q_HEADS = 2
ROT_HEADS = Q_HEADS + 1
HEADS = ROT_HEADS + 1
OUT_COLS = HEADS * HEAD

PACK = 4
PASSES = HID // (P * PACK)
PAIR = 2

TILES = 4
CHUNKS = BATCH * SEQ // (TILES * P)
SEQ_CHUNKS = SEQ // (TILES * P)
Q_VECTORS = TILES * Q_HEADS
ROT_VECTORS = TILES * ROT_HEADS

LOAD_AHEAD = 4
X_BUFS = LOAD_AHEAD + 2

FLOPS = 2 * BATCH * SEQ * HID * OUT_COLS


def tile_attention_pa_t_kernel(tc, x, cos, sin, Wq, Wk, Wv, out_0, out_1, out_2):
    nc = tc.nc

    by_chunk = "(c p j) n -> c p (j n)"
    x_chunks = x.flatten_outer_dims().rearrange(by_chunk, p=P, j=TILES)
    q_chunks = out_0.rearrange("b s h d -> (b s) (h d)").rearrange(by_chunk, p=P, j=TILES)
    k_chunks = out_1.rearrange("b s h d -> (b s) (h d)").rearrange(by_chunk, p=P, j=TILES)
    v_chunks = out_2.rearrange("b s h d -> (b s) (h d)").rearrange(by_chunk, p=P, j=TILES)

    with ExitStack() as stack:
        stack.enter_context(tc.manual_schedule())
        const = stack.enter_context(tc.tile_pool(name="const", bufs=1))
        x_pool = stack.enter_context(tc.tile_pool(name="x", bufs=X_BUFS))
        mx_pool = stack.enter_context(tc.tile_pool(name="mx", bufs=2))
        out_pool = stack.enter_context(tc.tile_pool(name="out", bufs=3))
        xt_psum = stack.enter_context(tc.psum_pool(name="xt_psum", bufs=TILES))
        head_psum = stack.enter_context(tc.psum_pool(name="head_psum", bufs=1))

        x_tiles, grouped_tiles, code_tiles, scale_tiles, head_tiles = {}, {}, {}, {}, {}

        def load(c, pieces=1):
            x_sb = x_pool.tile([P, TILES * HID], BF16, name="x_sb")
            width = TILES * HID // pieces
            for i in range(pieces):
                columns = slice(i * width, (i + 1) * width)
                nc.sync.dma_start(out=x_sb[:, columns], in_=x_chunks[c][:, columns])
            x_tiles[c] = x_sb

        def transpose(c):
            x_words = x_tiles[c][:].bitcast(F32)
            grouped = mx_pool.tile([P, TILES * HID], BF16, name="grouped", align_bytes=64)
            grouped_words = grouped[:].bitcast(F32).rearrange(
                "p (j g r u) -> p j g r u", j=TILES, g=PASSES, u=PAIR
            )
            for j in range(TILES):
                xt = xt_psum.tile([P, PASSES, PAIR, P], F32, name="xt")
                for g in range(PASSES):
                    for u in range(PAIR):
                        first = ((j * PASSES + g) * PAIR + u) * P
                        nc.tensor.transpose(
                            out=xt[:, g, u, :], in_=x_words[:, first : first + P], identity=ident[:]
                        )
                nc.scalar.copy(out=grouped_words[:, j], in_=xt[:].rearrange("p g u r -> p g r u"))
            grouped_tiles[c] = grouped

        def quantise(c):
            x_codes = mx_pool.tile([P, TILES * PASSES * P], U32, name="x_codes", align_bytes=64)
            x_scales = mx_pool.tile([P, TILES * PASSES * P], U8, name="x_scales", align_bytes=64)
            nc.vector.quantize_mx(
                out=x_codes[:].bitcast(FP8X4), scales=x_scales[:], in_=grouped_tiles[c][:]
            )
            code_tiles[c], scale_tiles[c] = x_codes, x_scales

        def project(c, h):
            acc = head_psum.tile([P, TILES, HEAD], F32, name="head%d" % h)
            for j in range(TILES):
                for g in range(PASSES):
                    tokens = slice((j * PASSES + g) * P, (j * PASSES + g + 1) * P)
                    columns = slice(g * OUT_COLS + h * HEAD, g * OUT_COLS + (h + 1) * HEAD)
                    nc.tensor.matmul_mx(
                        out=acc[:, j, :],
                        lhsT=code_tiles[c][:, tokens].bitcast(FP8X4),
                        lhsT_scale=scale_tiles[c][:, tokens],
                        rhs=w_codes[:, columns].bitcast(FP8X4),
                        rhs_scale=w_scales[:, columns],
                        start=(g == 0),
                        stop=(g == PASSES - 1),
                    )
            head_tiles[c, h] = acc

        def rotate_and_store(c):
            v_out = out_pool.tile([P, TILES, HEAD], F32, name="v_out")
            nc.scalar.copy(out=v_out[:], in_=head_tiles[c, ROT_HEADS][:])
            nc.sync.dma_start(out=v_chunks[c], in_=v_out[:].rearrange("p j d -> p (j d)"))

            products = out_pool.tile([P, 2, ROT_VECTORS, HEAD], F32, name="products")
            q_products = products[:, :, 0:Q_VECTORS, :].rearrange("p w (j h) d -> p w j h d", h=Q_HEADS)
            first = (c % SEQ_CHUNKS) * TILES
            for h in range(ROT_HEADS):
                nc.vector.tensor_tensor(
                    out=(
                        q_products[:, :, :, h, :]
                        if h < Q_HEADS
                        else products[:, :, Q_VECTORS:ROT_VECTORS, :]
                    ),
                    in0=head_tiles[c, h][:].unsqueeze(1).to_broadcast([P, 2, TILES, HEAD]),
                    in1=tables[:, :, first : first + TILES, :],
                    op=ALU.mult,
                )

            adder = nc.gpsimd if c < CHUNKS - 1 else nc.vector
            rot, cross = products[:, 0], products[:, 1]
            adder.tensor_tensor(
                out=rot[:, :, 0:HALF], in0=rot[:, :, 0:HALF], in1=cross[:, :, HALF:HEAD], op=ALU.subtract
            )
            adder.tensor_tensor(
                out=rot[:, :, HALF:HEAD], in0=rot[:, :, HALF:HEAD], in1=cross[:, :, 0:HALF], op=ALU.add
            )
            nc.sync.dma_start(out=q_chunks[c], in_=rot[:, 0:Q_VECTORS, :].rearrange("p n d -> p (n d)"))
            nc.sync.dma_start(
                out=k_chunks[c], in_=rot[:, Q_VECTORS:ROT_VECTORS, :].rearrange("p n d -> p (n d)")
            )

        ident = const.tile([P, P], F32)
        make_identity(nc, ident[:])

        w_raws = []
        for name, w in (("wq_raw", Wq), ("wk_raw", Wk), ("wv_raw", Wv)):
            w_raw = const.tile([P, PASSES, PACK, w.shape[1]], BF16, name=name)
            nc.sync.dma_start(
                out=w_raw[:].rearrange("p g (u e) n -> p (g u) (e n)", e=PAIR),
                in_=w.rearrange("(s q e) n -> q s (e n)", q=P, e=PAIR),
            )
            w_raws.append((w_raw, w.shape[1]))

        load(0, pieces=TILES)

        tables = const.tile([P, 2, SEQ_CHUNKS * TILES, HEAD], BF16)
        sin_sb = const.tile([P, SEQ_CHUNKS * TILES, HEAD], BF16)
        for table_sb, table in ((sin_sb[:], sin), (tables[:, 0], cos)):
            nc.sync.dma_start(
                out=table_sb.rearrange("p (c j) d -> p c (j d)", j=TILES),
                in_=table.rearrange("(c p j) d -> p c (j d)", p=P, j=TILES),
            )

        for c in range(1, LOAD_AHEAD):
            load(c)

        w_grouped = const.tile([P, PASSES, OUT_COLS, PACK], BF16, align_bytes=64)
        w_first = 0
        for w_raw, w_cols in w_raws:
            for g in range(PASSES):
                nc.vector.tensor_copy(
                    out=w_grouped[:, g, w_first : w_first + w_cols, :],
                    in_=w_raw[:, g].rearrange("p t n -> p n t"),
                )
            w_first += w_cols
        w_codes = const.tile([P, PASSES * OUT_COLS], U32, align_bytes=64)
        w_scales = const.tile([P, PASSES * OUT_COLS], U8, align_bytes=64)
        nc.vector.quantize_mx(
            out=w_codes[:].bitcast(FP8X4),
            scales=w_scales[:],
            in_=w_grouped[:].rearrange("p g n t -> p (g n t)"),
        )

        transpose(0)
        transpose(1)

        nc.scalar.copy(out=tables[:, 1, :, 0:HALF], in_=sin_sb[:, :, HALF:HEAD])
        nc.scalar.copy(out=tables[:, 1, :, HALF:HEAD], in_=sin_sb[:, :, 0:HALF])

        quantise(0)
        for c in range(CHUNKS):
            if c + LOAD_AHEAD < CHUNKS:
                load(c + LOAD_AHEAD)
            if c + 1 < CHUNKS:
                quantise(c + 1)
            for h in range(Q_HEADS):
                project(c, h)
            if c + 2 < CHUNKS:
                transpose(c + 2)
            for h in range(Q_HEADS, HEADS):
                project(c, h)
            rotate_and_store(c)
